import numpy as np
import ml_dtypes


def mxq(x, axis, fmt="e4m3"):
    dtype, down = {"e4m3": (ml_dtypes.float8_e4m3fn, 7), "e5m2": (ml_dtypes.float8_e5m2, 14)}[fmt]
    v = np.moveaxis(np.asarray(x, np.float32).astype(ml_dtypes.bfloat16).astype(np.float64), axis, -1)
    blocks = v.reshape(v.shape[:-1] + (-1, 32))
    amax = np.abs(blocks).max(-1, keepdims=True)
    byte = np.maximum(np.where(amax > 0, np.frexp(amax)[1] - 1 + 127, 0) - down, 1)
    scale = np.exp2(byte - 127.0)
    codes = (blocks / scale).astype(np.float32).astype(dtype).astype(np.float64)
    return np.moveaxis((codes * scale).reshape(v.shape), -1, axis)


WIDE = False


def mx_kscale(k):
    if not WIDE:
        return np.ones(k)
    levels = np.array([10, -10, 5, -5, 0])
    a = np.random.permutation(np.resize(levels, k // 512 * 4)).reshape(k // 512, 4)
    idx = np.arange(k)
    return np.exp2(a[idx // 512, idx % 128 // 32])


BF16 = ml_dtypes.bfloat16


def bf(x):
    return np.asarray(x, np.float32).astype(BF16)


def f64(x):
    return np.asarray(x).astype(np.float64)


B, S, D, N = 4, 2048, 512, 128
EPS = 1e-6
GS = 6.0 / np.sqrt(D)
LEVELS = np.array([-1.0, -0.5, 0.0, 0.5, 1.0])
PROBS = np.array([0.23, 0.17, 0.2, 0.17, 0.23])


def setup_inputs():
    s = mx_kscale(D)
    s2 = np.concatenate([s, s])
    return {"x_real": bf(np.random.standard_normal((B, S, D)) * 1.2 + 0.5),
            "x_imag": bf(np.random.standard_normal((B, S, D)) * 0.7 + 0.1),
            "qw_re": bf(np.random.choice(LEVELS, size=(N, D), p=PROBS) / s),
            "qw_im": bf(np.random.choice(LEVELS, size=(N, D), p=PROBS) / s),
            "gamma": bf((1.0 + 0.1 * np.random.standard_normal(D + D)) * GS * s2),
            "beta": bf(0.2 * np.random.standard_normal(D + D) * GS * s2),
            "s_re": bf(0.7 + 0.05 * np.random.standard_normal(1)),
            "s_im": bf(0.9 + 0.05 * np.random.standard_normal(1))}


def reference(x_real, x_imag, qw_re, qw_im, gamma, beta, s_re, s_im):
    x_cat = np.concatenate([f64(x_real), f64(x_imag)], axis=-1)
    mu = x_cat.mean(axis=-1, keepdims=True)
    var = x_cat.var(axis=-1, keepdims=True)
    norm = (x_cat - mu) * (1.0 / np.sqrt(var + EPS)) * f64(gamma) + f64(beta)
    nr = mxq(norm[..., :D], 2, "e4m3")
    ni = mxq(norm[..., D:], 2, "e4m3")
    wr = mxq(f64(qw_re), 1, "e4m3").T
    wi = mxq(f64(qw_im), 1, "e4m3").T
    y_real = (nr @ wr) - (ni @ wi)
    y_imag = (nr @ wi) + (ni @ wr)
    return y_real * f64(s_re), y_imag * f64(s_im)

@@ -1,0 +1,191 @@
+from contextlib import ExitStack
+
+import concourse.mybir as mybir
+from concourse.masks import make_identity
+
+F32 = mybir.dt.float32
+BF16 = mybir.dt.bfloat16
+U32 = mybir.dt.uint32
+U8 = mybir.dt.uint8
+FP8X4 = mybir.dt.float8_e4m3fn_x4
+ACT = mybir.ActivationFunctionType
+ALU = mybir.AluOpType
+
+P = 128
+PACK = 4
+ROWS = 4 * 2048
+D = 512
+N_OUT = 128
+HALVES = 2
+K_BLOCKS = HALVES * D // P
+EPS = 1e-6
+
+LOAD_TILES = 8
+GROUP_TILES = 4
+GROUP_ROWS = GROUP_TILES * P
+LOADS = ROWS // (LOAD_TILES * P)
+GROUPS_PER_LOAD = LOAD_TILES // GROUP_TILES
+VECTOR_NORM_TILES = 1
+
+FLOPS = 4 * 2 * ROWS * D * N_OUT
+
+
+def tile_realimagfourvallinear_pa_t_kernel(
+    tc, x_real, x_imag, qw_re, qw_im, gamma, beta, s_re, s_im, out_0, out_1
+):
+    nc = tc.nc
+    x_views = [
+        x.flatten_outer_dims().rearrange("(s p j) k -> s p j k", p=P, j=LOAD_TILES)
+        for x in (x_real, x_imag)
+    ]
+    y_views = [
+        y.flatten_outer_dims().rearrange("(s p j) n -> s p j n", p=P, j=LOAD_TILES)
+        for y in (out_0, out_1)
+    ]
+
+    with ExitStack() as ctx:
+        const = ctx.enter_context(tc.tile_pool(name="const", bufs=1))
+        x_pool = ctx.enter_context(tc.tile_pool(name="x_pool", bufs=LOADS))
+
+        x_tiles = []
+        for s in range(LOADS):
+            x_sb = x_pool.tile([P, HALVES, LOAD_TILES, D], BF16)
+            for h in range(HALVES):
+                nc.sync.dma_start(out=x_sb[:, h], in_=x_views[h][s])
+            x_tiles.append(x_sb)
+
+        ident_f32 = const.tile([P, P], F32)
+        make_identity(nc, ident_f32[:])
+        eps_col = const.tile([P, 1], F32)
+        nc.vector.memset(eps_col[:], EPS)
+        gain_cols = const.tile([P, HALVES], F32)
+        affine_cols = const.tile([P, 2 * K_BLOCKS], F32)
+        w_codes = const.tile([P, HALVES * 2 * N_OUT], U32, align_bytes=64)
+        w_scales = const.tile([P, HALVES * 2 * N_OUT], U8, align_bytes=64)
+
+        with tc.tile_pool(name="setup", bufs=1) as setup, tc.psum_pool(name="setup_psum", bufs=1) as setup_psum:
+            ident_bf16 = setup.tile([P, P], BF16)
+            make_identity(nc, ident_bf16[:])
+
+            s_re_bf16 = setup.tile([P, 1], BF16)
+            s_im_bf16 = setup.tile([P, 1], BF16)
+            nc.scalar.dma_start(out=s_re_bf16[:], in_=s_re.partition_broadcast(P))
+            nc.scalar.dma_start(out=s_im_bf16[:], in_=s_im.partition_broadcast(P))
+            nc.vector.tensor_copy(out=gain_cols[:, 0:1], in_=s_re_bf16[:])
+            nc.vector.tensor_copy(out=gain_cols[:, 1:2], in_=s_im_bf16[:])
+
+            affine_rows = setup.tile([P, P], BF16)
+            nc.vector.memset(affine_rows[:], 0.0)
+            nc.scalar.dma_start(out=affine_rows[0:K_BLOCKS, :], in_=gamma.rearrange("(b c) -> b c", c=P))
+            nc.scalar.dma_start(out=affine_rows[K_BLOCKS : 2 * K_BLOCKS, :], in_=beta.rearrange("(b c) -> b c", c=P))
+            affine_t = setup_psum.tile([P, P], BF16)
+            nc.tensor.transpose(affine_t[:], affine_rows[:], ident_bf16[:])
+            nc.vector.tensor_copy(out=affine_cols[:], in_=affine_t[:, 0 : 2 * K_BLOCKS])
+
+            w_t = []
+            for w in (qw_re, qw_im):
+                w_sb = setup.tile([P, D], BF16, name="w_sb", bufs=2)
+                nc.scalar.dma_start(out=w_sb[:], in_=w)
+                w_ps = setup_psum.tile([P, PACK, N_OUT], BF16, name="w_ps", bufs=2)
+                for t in range(PACK):
+                    nc.tensor.transpose(w_ps[:, t, :], w_sb[:, t * P : (t + 1) * P], ident_bf16[:])
+                w_t.append(w_ps[:].rearrange("p t n -> p n t"))
+            w_grouped = setup.tile([P, HALVES * 2, N_OUT, PACK], BF16, align_bytes=64)
+            nc.vector.tensor_copy(out=w_grouped[:, 0], in_=w_t[0])
+            nc.vector.tensor_copy(out=w_grouped[:, 1], in_=w_t[1])
+            nc.vector.tensor_scalar_mul(out=w_grouped[:, 2], in0=w_t[1], scalar1=-1.0)
+            nc.vector.tensor_copy(out=w_grouped[:, 3], in_=w_t[0])
+            nc.vector.quantize_mx(
+                out=w_codes[:].bitcast(FP8X4),
+                scales=w_scales[:],
+                in_=w_grouped[:].rearrange("p q n t -> p (q n t)"),
+            )
+
+        small = ctx.enter_context(tc.tile_pool(name="small", bufs=4))
+        work = ctx.enter_context(tc.tile_pool(name="work", bufs=2))
+        t_psum = ctx.enter_context(tc.psum_pool(name="t_psum", bufs=6))
+        y_psum = ctx.enter_context(tc.psum_pool(name="y_psum", bufs=2))
+
+        for g in range(LOADS * GROUPS_PER_LOAD):
+            s, first_tile = g // GROUPS_PER_LOAD, (g % GROUPS_PER_LOAD) * GROUP_TILES
+            x_sb = x_tiles[s]
+
+            stats = small.tile([P, GROUP_TILES, HALVES, 6], F32)
+            mean_var = small.tile([P, GROUP_TILES, 2], F32)
+            for j in range(GROUP_TILES):
+                for h in range(HALVES):
+                    nc.vector.bn_stats(out=stats[:, j, h, :], in_=x_sb[:, h, first_tile + j, :])
+                nc.vector.bn_aggr(out=mean_var[:, j, :], in_=stats[:, j].rearrange("p h c -> p (h c)"))
+            std = small.tile([P, GROUP_TILES], F32)
+            nc.scalar.activation(out=std[:], in_=mean_var[:, :, 1], func=ACT.Sqrt, bias=eps_col[:], scale=1.0)
+            rstd = small.tile([P, GROUP_TILES], F32)
+            nc.vector.reciprocal(out=rstd[:], in_=std[:])
+            shift = small.tile([P, GROUP_TILES], F32)
+            nc.vector.scalar_tensor_tensor(
+                out=shift[:], in0=mean_var[:, :, 0], scalar=-1.0, in1=rstd[:], op0=ALU.mult, op1=ALU.mult
+            )
+
+            x_hat = work.tile([P, GROUP_TILES, HALVES, D], F32)
+            for j in range(GROUP_TILES):
+                if j < VECTOR_NORM_TILES:
+                    nc.vector.tensor_scalar(
+                        out=x_hat[:, j], in0=x_sb[:, :, first_tile + j, :],
+                        scalar1=rstd[:, j : j + 1], scalar2=shift[:, j : j + 1], op0=ALU.mult, op1=ALU.add,
+                    )
+                else:
+                    nc.scalar.activation(
+                        out=x_hat[:, j], in_=x_sb[:, :, first_tile + j, :], func=ACT.Identity,
+                        scale=rstd[:, j : j + 1], bias=shift[:, j : j + 1],
+                    )
+
+            planes = work.tile([P, K_BLOCKS, GROUP_ROWS], BF16)
+            for b in range(K_BLOCKS):
+                h, t = b // PACK, b % PACK
+                x_hat_t = t_psum.tile([P, GROUP_ROWS], F32)
+                for j in range(GROUP_TILES):
+                    nc.tensor.transpose(
+                        x_hat_t[:, j * P : (j + 1) * P], x_hat[:, j, h, t * P : (t + 1) * P], ident_f32[:]
+                    )
+                nc.scalar.activation(
+                    out=planes[:, b, :], in_=x_hat_t[:], func=ACT.Identity,
+                    scale=affine_cols[:, b : b + 1], bias=affine_cols[:, K_BLOCKS + b : K_BLOCKS + b + 1],
+                )
+
+            grouped = work.tile([P, HALVES, GROUP_ROWS, PACK], BF16, align_bytes=64)
+            codes = work.tile([P, HALVES, GROUP_ROWS], U32, align_bytes=64)
+            scales = work.tile([P, HALVES, GROUP_ROWS], U8, align_bytes=64)
+            for h in range(HALVES):
+                nc.vector.tensor_copy(
+                    out=grouped[:, h].rearrange("p (c i) t -> p c t i", i=4),
+                    in_=planes[:, h * PACK : (h + 1) * PACK, :].rearrange("p t (c i) -> p c t i", i=4),
+                )
+            for h in range(HALVES):
+                nc.vector.quantize_mx(
+                    out=codes[:, h, :].bitcast(FP8X4),
+                    scales=scales[:, h, :],
+                    in_=grouped[:, h].rearrange("p r t -> p (r t)"),
+                )
+
+            y_sb = [work.tile([P, GROUP_TILES, N_OUT], F32, name="y_sb_%d" % c) for c in range(HALVES)]
+            for pair in range(GROUP_TILES // 2):
+                y_ps = y_psum.tile([P, 2, HALVES * N_OUT], F32)
+                for i in range(2):
+                    rows = slice((2 * pair + i) * P, (2 * pair + i + 1) * P)
+                    for h in range(HALVES):
+                        cols = slice(h * 2 * N_OUT, (h + 1) * 2 * N_OUT)
+                        nc.tensor.matmul_mx(
+                            out=y_ps[:, i, :],
+                            lhsT=codes[:, h, rows].bitcast(FP8X4),
+                            lhsT_scale=scales[:, h, rows],
+                            rhs=w_codes[:, cols].bitcast(FP8X4),
+                            rhs_scale=w_scales[:, cols],
+                            start=(h == 0),
+                            stop=(h == HALVES - 1),
+                        )
+                for c in range(HALVES):
+                    nc.scalar.activation(
+                        out=y_sb[c][:, 2 * pair : 2 * pair + 2, :], in_=y_ps[:, :, c * N_OUT : (c + 1) * N_OUT],
+                        func=ACT.Copy, scale=gain_cols[:, c : c + 1],
+                    )
+            for c in range(HALVES):
+                nc.sync.dma_start(out=y_views[c][s][:, first_tile : first_tile + GROUP_TILES, :], in_=y_sb[c][:])

@@ -20,12 +20,9 @@ HALVES = 2
 K_BLOCKS = HALVES * D // P
 EPS = 1e-6
 
-LOAD_TILES = 8
 GROUP_TILES = 4
 GROUP_ROWS = GROUP_TILES * P
-LOADS = ROWS // (LOAD_TILES * P)
-GROUPS_PER_LOAD = LOAD_TILES // GROUP_TILES
-VECTOR_NORM_TILES = 1
+GROUPS = ROWS // GROUP_ROWS
 
 FLOPS = 4 * 2 * ROWS * D * N_OUT
 
@@ -35,29 +32,29 @@ def tile_realimagfourvallinear_pa_t_kernel(
 ):
     nc = tc.nc
     x_views = [
-        x.flatten_outer_dims().rearrange("(s p j) k -> s p j k", p=P, j=LOAD_TILES)
+        x.flatten_outer_dims().rearrange("(g p j) k -> g p j k", p=P, j=GROUP_TILES)
         for x in (x_real, x_imag)
     ]
     y_views = [
-        y.flatten_outer_dims().rearrange("(s p j) n -> s p j n", p=P, j=LOAD_TILES)
+        y.flatten_outer_dims().rearrange("(g p j) n -> g p j n", p=P, j=GROUP_TILES)
         for y in (out_0, out_1)
     ]
 
     with ExitStack() as ctx:
         const = ctx.enter_context(tc.tile_pool(name="const", bufs=1))
-        x_pool = ctx.enter_context(tc.tile_pool(name="x_pool", bufs=LOADS))
+        x_pool = ctx.enter_context(tc.tile_pool(name="x_pool", bufs=GROUPS))
 
         x_tiles = []
-        for s in range(LOADS):
-            x_sb = x_pool.tile([P, HALVES, LOAD_TILES, D], BF16)
+        for g in range(GROUPS):
+            x_sb = x_pool.tile([P, HALVES, GROUP_TILES, D], BF16)
             for h in range(HALVES):
-                nc.sync.dma_start(out=x_sb[:, h], in_=x_views[h][s])
+                nc.sync.dma_start(out=x_sb[:, h], in_=x_views[h][g])
             x_tiles.append(x_sb)
 
         ident_f32 = const.tile([P, P], F32)
         make_identity(nc, ident_f32[:])
-        eps_col = const.tile([P, 1], F32)
-        nc.vector.memset(eps_col[:], EPS)
+        minus_half = const.tile([P, GROUP_TILES], F32)
+        nc.vector.memset(minus_half[:], -0.5)
         gain_cols = const.tile([P, HALVES], F32)
         affine_cols = const.tile([P, 2 * K_BLOCKS], F32)
         w_codes = const.tile([P, HALVES * 2 * N_OUT], U32, align_bytes=64)
@@ -106,86 +103,122 @@ def tile_realimagfourvallinear_pa_t_kernel(
         t_psum = ctx.enter_context(tc.psum_pool(name="t_psum", bufs=6))
         y_psum = ctx.enter_context(tc.psum_pool(name="y_psum", bufs=2))
 
-        for g in range(LOADS * GROUPS_PER_LOAD):
-            s, first_tile = g // GROUPS_PER_LOAD, (g % GROUPS_PER_LOAD) * GROUP_TILES
-            x_sb = x_tiles[s]
+        mean_var, rstd, shift, x_hat, planes, codes, scales, y_ps = ({} for i in range(8))
 
+        def statistics(g):
             stats = small.tile([P, GROUP_TILES, HALVES, 6], F32)
-            mean_var = small.tile([P, GROUP_TILES, 2], F32)
+            mean_var[g] = small.tile([P, GROUP_TILES, 2], F32, name="mean_var")
             for j in range(GROUP_TILES):
                 for h in range(HALVES):
-                    nc.vector.bn_stats(out=stats[:, j, h, :], in_=x_sb[:, h, first_tile + j, :])
-                nc.vector.bn_aggr(out=mean_var[:, j, :], in_=stats[:, j].rearrange("p h c -> p (h c)"))
-            std = small.tile([P, GROUP_TILES], F32)
-            nc.scalar.activation(out=std[:], in_=mean_var[:, :, 1], func=ACT.Sqrt, bias=eps_col[:], scale=1.0)
-            rstd = small.tile([P, GROUP_TILES], F32)
-            nc.vector.reciprocal(out=rstd[:], in_=std[:])
-            shift = small.tile([P, GROUP_TILES], F32)
-            nc.vector.scalar_tensor_tensor(
-                out=shift[:], in0=mean_var[:, :, 0], scalar=-1.0, in1=rstd[:], op0=ALU.mult, op1=ALU.mult
+                    nc.vector.bn_stats(out=stats[:, j, h, :], in_=x_tiles[g][:, h, j, :])
+                nc.vector.bn_aggr(out=mean_var[g][:, j, :], in_=stats[:, j].rearrange("p h c -> p (h c)"))
+
+        def scale_and_shift(g):
+            var_eps = small.tile([P, GROUP_TILES], F32)
+            nc.gpsimd.tensor_scalar(
+                out=var_eps[:], in0=mean_var[g][:, :, 1], scalar1=1.0, scalar2=EPS, op0=ALU.mult, op1=ALU.add
             )
+            rstd[g] = small.tile([P, GROUP_TILES], F32, name="rstd")
+            nc.gpsimd.tensor_tensor(out=rstd[g][:], in0=var_eps[:], in1=minus_half[:], op=ALU.pow)
+            neg_mean = small.tile([P, GROUP_TILES], F32)
+            nc.gpsimd.tensor_scalar(
+                out=neg_mean[:], in0=mean_var[g][:, :, 0], scalar1=-1.0, scalar2=0.0, op0=ALU.mult, op1=ALU.add
+            )
+            shift[g] = small.tile([P, GROUP_TILES], F32, name="shift")
+            nc.gpsimd.tensor_tensor(out=shift[g][:], in0=neg_mean[:], in1=rstd[g][:], op=ALU.mult)
 
-            x_hat = work.tile([P, GROUP_TILES, HALVES, D], F32)
-            for j in range(GROUP_TILES):
-                if j < VECTOR_NORM_TILES:
-                    nc.vector.tensor_scalar(
-                        out=x_hat[:, j], in0=x_sb[:, :, first_tile + j, :],
-                        scalar1=rstd[:, j : j + 1], scalar2=shift[:, j : j + 1], op0=ALU.mult, op1=ALU.add,
-                    )
-                else:
-                    nc.scalar.activation(
-                        out=x_hat[:, j], in_=x_sb[:, :, first_tile + j, :], func=ACT.Identity,
-                        scale=rstd[:, j : j + 1], bias=shift[:, j : j + 1],
-                    )
+        def normalise(g, j):
+            if j == 0:
+                x_hat[g] = work.tile([P, GROUP_TILES, HALVES, D], F32, name="x_hat")
+            if j % 2 == 0:
+                nc.scalar.activation(
+                    out=x_hat[g][:, j], in_=x_tiles[g][:, :, j, :], func=ACT.Identity,
+                    scale=rstd[g][:, j : j + 1], bias=shift[g][:, j : j + 1],
+                )
+            else:
+                nc.gpsimd.tensor_scalar(
+                    out=x_hat[g][:, j], in0=x_tiles[g][:, :, j, :],
+                    scalar1=rstd[g][:, j : j + 1], scalar2=shift[g][:, j : j + 1], op0=ALU.mult, op1=ALU.add,
+                )
 
-            planes = work.tile([P, K_BLOCKS, GROUP_ROWS], BF16)
-            for b in range(K_BLOCKS):
-                h, t = b // PACK, b % PACK
+        def transpose_and_affine(g, h):
+            if h == 0:
+                planes[g] = work.tile([P, K_BLOCKS, GROUP_ROWS], BF16, name="planes")
+            for t in range(PACK):
+                b = h * PACK + t
                 x_hat_t = t_psum.tile([P, GROUP_ROWS], F32)
                 for j in range(GROUP_TILES):
                     nc.tensor.transpose(
-                        x_hat_t[:, j * P : (j + 1) * P], x_hat[:, j, h, t * P : (t + 1) * P], ident_f32[:]
+                        x_hat_t[:, j * P : (j + 1) * P], x_hat[g][:, j, h, t * P : (t + 1) * P], ident_f32[:]
                     )
                 nc.scalar.activation(
-                    out=planes[:, b, :], in_=x_hat_t[:], func=ACT.Identity,
+                    out=planes[g][:, b, :], in_=x_hat_t[:], func=ACT.Identity,
                     scale=affine_cols[:, b : b + 1], bias=affine_cols[:, K_BLOCKS + b : K_BLOCKS + b + 1],
                 )
 
+        def quantise(g):
             grouped = work.tile([P, HALVES, GROUP_ROWS, PACK], BF16, align_bytes=64)
-            codes = work.tile([P, HALVES, GROUP_ROWS], U32, align_bytes=64)
-            scales = work.tile([P, HALVES, GROUP_ROWS], U8, align_bytes=64)
+            codes[g] = work.tile([P, HALVES, GROUP_ROWS], U32, align_bytes=64, name="codes")
+            scales[g] = work.tile([P, HALVES, GROUP_ROWS], U8, align_bytes=64, name="scales")
             for h in range(HALVES):
                 nc.vector.tensor_copy(
                     out=grouped[:, h].rearrange("p (c i) t -> p c t i", i=4),
-                    in_=planes[:, h * PACK : (h + 1) * PACK, :].rearrange("p t (c i) -> p c t i", i=4),
+                    in_=planes[g][:, h * PACK : (h + 1) * PACK, :].rearrange("p t (c i) -> p c t i", i=4),
                 )
             for h in range(HALVES):
                 nc.vector.quantize_mx(
-                    out=codes[:, h, :].bitcast(FP8X4),
-                    scales=scales[:, h, :],
+                    out=codes[g][:, h, :].bitcast(FP8X4),
+                    scales=scales[g][:, h, :],
                     in_=grouped[:, h].rearrange("p r t -> p (r t)"),
                 )
 
-            y_sb = [work.tile([P, GROUP_TILES, N_OUT], F32, name="y_sb_%d" % c) for c in range(HALVES)]
+        def multiply(g):
+            y_ps[g] = []
             for pair in range(GROUP_TILES // 2):
-                y_ps = y_psum.tile([P, 2, HALVES * N_OUT], F32)
+                y_pair = y_psum.tile([P, 2, HALVES * N_OUT], F32)
                 for i in range(2):
                     rows = slice((2 * pair + i) * P, (2 * pair + i + 1) * P)
                     for h in range(HALVES):
                         cols = slice(h * 2 * N_OUT, (h + 1) * 2 * N_OUT)
                         nc.tensor.matmul_mx(
-                            out=y_ps[:, i, :],
-                            lhsT=codes[:, h, rows].bitcast(FP8X4),
-                            lhsT_scale=scales[:, h, rows],
+                            out=y_pair[:, i, :],
+                            lhsT=codes[g][:, h, rows].bitcast(FP8X4),
+                            lhsT_scale=scales[g][:, h, rows],
                             rhs=w_codes[:, cols].bitcast(FP8X4),
                             rhs_scale=w_scales[:, cols],
                             start=(h == 0),
                             stop=(h == HALVES - 1),
                         )
-                for c in range(HALVES):
+                y_ps[g].append(y_pair)
+
+        def gains_and_store(g):
+            for c in range(HALVES):
+                y_sb = work.tile([P, GROUP_TILES, N_OUT], F32, name="y_sb_%d" % c)
+                for pair in range(GROUP_TILES // 2):
                     nc.scalar.activation(
-                        out=y_sb[c][:, 2 * pair : 2 * pair + 2, :], in_=y_ps[:, :, c * N_OUT : (c + 1) * N_OUT],
+                        out=y_sb[:, 2 * pair : 2 * pair + 2, :], in_=y_ps[g][pair][:, :, c * N_OUT : (c + 1) * N_OUT],
                         func=ACT.Copy, scale=gain_cols[:, c : c + 1],
                     )
-            for c in range(HALVES):
-                nc.sync.dma_start(out=y_views[c][s][:, first_tile : first_tile + GROUP_TILES, :], in_=y_sb[c][:])
+                nc.sync.dma_start(out=y_views[c][g], in_=y_sb[:])
+
+        def in_range(g):
+            return 0 <= g < GROUPS
+
+        with tc.manual_schedule():
+            for s in range(-2, GROUPS + 2):
+                if in_range(s - 1):
+                    quantise(s - 1)
+                if in_range(s + 2):
+                    statistics(s + 2)
+                if in_range(s - 2):
+                    gains_and_store(s - 2)
+                for h in range(HALVES):
+                    if in_range(s):
+                        transpose_and_affine(s, h)
+                    if in_range(s + 1):
+                        normalise(s + 1, 2 * h)
+                        normalise(s + 1, 2 * h + 1)
+                if in_range(s + 2):
+                    scale_and_shift(s + 2)
+                if in_range(s - 1):
+                    multiply(s - 1)

@@ -103,47 +103,35 @@ def tile_realimagfourvallinear_pa_t_kernel(
         t_psum = ctx.enter_context(tc.psum_pool(name="t_psum", bufs=6))
         y_psum = ctx.enter_context(tc.psum_pool(name="y_psum", bufs=2))
 
-        mean_var, rstd, shift, x_hat, planes, codes, scales, y_ps = ({} for i in range(8))
+        neg_mean, var_eps, rstd, x_hat, planes, grouped, codes, scales, y_ps = ({} for i in range(9))
 
         def statistics(g):
             stats = small.tile([P, GROUP_TILES, HALVES, 6], F32)
-            mean_var[g] = small.tile([P, GROUP_TILES, 2], F32, name="mean_var")
+            mean_var = small.tile([P, GROUP_TILES, 2], F32)
             for j in range(GROUP_TILES):
                 for h in range(HALVES):
                     nc.vector.bn_stats(out=stats[:, j, h, :], in_=x_tiles[g][:, h, j, :])
-                nc.vector.bn_aggr(out=mean_var[g][:, j, :], in_=stats[:, j].rearrange("p h c -> p (h c)"))
+            for j in range(GROUP_TILES):
+                nc.vector.bn_aggr(out=mean_var[:, j, :], in_=stats[:, j].rearrange("p h c -> p (h c)"))
+            neg_mean[g] = small.tile([P, GROUP_TILES], F32, name="neg_mean")
+            nc.vector.tensor_scalar_mul(out=neg_mean[g][:], in0=mean_var[:, :, 0], scalar1=-1.0)
+            var_eps[g] = small.tile([P, GROUP_TILES], F32, name="var_eps")
+            nc.vector.tensor_scalar_add(out=var_eps[g][:], in0=mean_var[:, :, 1], scalar1=EPS)
 
-        def scale_and_shift(g):
-            var_eps = small.tile([P, GROUP_TILES], F32)
-            nc.gpsimd.tensor_scalar(
-                out=var_eps[:], in0=mean_var[g][:, :, 1], scalar1=1.0, scalar2=EPS, op0=ALU.mult, op1=ALU.add
-            )
+        def reciprocal_std(g):
             rstd[g] = small.tile([P, GROUP_TILES], F32, name="rstd")
-            nc.gpsimd.tensor_tensor(out=rstd[g][:], in0=var_eps[:], in1=minus_half[:], op=ALU.pow)
-            neg_mean = small.tile([P, GROUP_TILES], F32)
-            nc.gpsimd.tensor_scalar(
-                out=neg_mean[:], in0=mean_var[g][:, :, 0], scalar1=-1.0, scalar2=0.0, op0=ALU.mult, op1=ALU.add
-            )
-            shift[g] = small.tile([P, GROUP_TILES], F32, name="shift")
-            nc.gpsimd.tensor_tensor(out=shift[g][:], in0=neg_mean[:], in1=rstd[g][:], op=ALU.mult)
+            nc.gpsimd.tensor_tensor(out=rstd[g][:], in0=var_eps[g][:], in1=minus_half[:], op=ALU.pow)
 
-        def normalise(g, j):
-            if j == 0:
-                x_hat[g] = work.tile([P, GROUP_TILES, HALVES, D], F32, name="x_hat")
-            if j % 2 == 0:
-                nc.scalar.activation(
-                    out=x_hat[g][:, j], in_=x_tiles[g][:, :, j, :], func=ACT.Identity,
-                    scale=rstd[g][:, j : j + 1], bias=shift[g][:, j : j + 1],
-                )
-            else:
+        def normalise(g):
+            x_hat[g] = work.tile([P, GROUP_TILES, HALVES, D], F32, name="x_hat")
+            for j in range(GROUP_TILES):
                 nc.gpsimd.tensor_scalar(
                     out=x_hat[g][:, j], in0=x_tiles[g][:, :, j, :],
-                    scalar1=rstd[g][:, j : j + 1], scalar2=shift[g][:, j : j + 1], op0=ALU.mult, op1=ALU.add,
+                    scalar1=neg_mean[g][:, j : j + 1], scalar2=rstd[g][:, j : j + 1], op0=ALU.add, op1=ALU.mult,
                 )
 
         def transpose_and_affine(g, h):
-            if h == 0:
-                planes[g] = work.tile([P, K_BLOCKS, GROUP_ROWS], BF16, name="planes")
+            planes[g, h] = work.tile([P, PACK, GROUP_ROWS], BF16, name="planes_%d" % h)
             for t in range(PACK):
                 b = h * PACK + t
                 x_hat_t = t_psum.tile([P, GROUP_ROWS], F32)
@@ -152,24 +140,27 @@ def tile_realimagfourvallinear_pa_t_kernel(
                         x_hat_t[:, j * P : (j + 1) * P], x_hat[g][:, j, h, t * P : (t + 1) * P], ident_f32[:]
                     )
                 nc.scalar.activation(
-                    out=planes[g][:, b, :], in_=x_hat_t[:], func=ACT.Identity,
+                    out=planes[g, h][:, t, :], in_=x_hat_t[:], func=ACT.Identity,
                     scale=affine_cols[:, b : b + 1], bias=affine_cols[:, K_BLOCKS + b : K_BLOCKS + b + 1],
                 )
 
+        def regroup(g, h):
+            grouped[g, h] = work.tile([P, GROUP_ROWS, PACK], BF16, align_bytes=64, name="grouped_%d" % h)
+            side_by_side = grouped[g, h][:].rearrange("p (c i) t -> p c t i", i=4)
+            plane_by_plane = planes[g, h][:].rearrange("p t (c i) -> p c t i", i=4)
+            if h == 0:
+                nc.vector.tensor_copy(out=side_by_side, in_=plane_by_plane)
+            else:
+                nc.scalar.copy(out=side_by_side, in_=plane_by_plane)
+
         def quantise(g):
-            grouped = work.tile([P, HALVES, GROUP_ROWS, PACK], BF16, align_bytes=64)
             codes[g] = work.tile([P, HALVES, GROUP_ROWS], U32, align_bytes=64, name="codes")
             scales[g] = work.tile([P, HALVES, GROUP_ROWS], U8, align_bytes=64, name="scales")
-            for h in range(HALVES):
-                nc.vector.tensor_copy(
-                    out=grouped[:, h].rearrange("p (c i) t -> p c t i", i=4),
-                    in_=planes[g][:, h * PACK : (h + 1) * PACK, :].rearrange("p t (c i) -> p c t i", i=4),
-                )
             for h in range(HALVES):
                 nc.vector.quantize_mx(
                     out=codes[g][:, h, :].bitcast(FP8X4),
                     scales=scales[g][:, h, :],
-                    in_=grouped[:, h].rearrange("p r t -> p (r t)"),
+                    in_=grouped[g, h][:].rearrange("p r t -> p (r t)"),
                 )
 
         def multiply(g):
@@ -207,18 +198,21 @@ def tile_realimagfourvallinear_pa_t_kernel(
         with tc.manual_schedule():
             for s in range(-2, GROUPS + 2):
                 if in_range(s - 1):
-                    quantise(s - 1)
+                    regroup(s - 1, 0)
                 if in_range(s + 2):
                     statistics(s + 2)
+                if in_range(s - 1):
+                    quantise(s - 1)
+                if in_range(s - 2):
+                    multiply(s - 2)
+                if in_range(s):
+                    transpose_and_affine(s, 0)
                 if in_range(s - 2):
                     gains_and_store(s - 2)
-                for h in range(HALVES):
-                    if in_range(s):
-                        transpose_and_affine(s, h)
-                    if in_range(s + 1):
-                        normalise(s + 1, 2 * h)
-                        normalise(s + 1, 2 * h + 1)
+                if in_range(s):
+                    transpose_and_affine(s, 1)
+                    regroup(s, 1)
+                if in_range(s + 1):
+                    normalise(s + 1)
                 if in_range(s + 2):
-                    scale_and_shift(s + 2)
-                if in_range(s - 1):
-                    multiply(s - 1)
+                    reciprocal_std(s + 2)

@@ -23,6 +23,7 @@ EPS = 1e-6
 GROUP_TILES = 4
 GROUP_ROWS = GROUP_TILES * P
 GROUPS = ROWS // GROUP_ROWS
+VECTOR_NORM_TILES = 1
 
 FLOPS = 4 * 2 * ROWS * D * N_OUT
 
@@ -108,8 +109,8 @@ def tile_realimagfourvallinear_pa_t_kernel(
         def statistics(g):
             stats = small.tile([P, GROUP_TILES, HALVES, 6], F32)
             mean_var = small.tile([P, GROUP_TILES, 2], F32)
-            for j in range(GROUP_TILES):
-                for h in range(HALVES):
+            for h in range(HALVES):
+                for j in range(GROUP_TILES):
                     nc.vector.bn_stats(out=stats[:, j, h, :], in_=x_tiles[g][:, h, j, :])
             for j in range(GROUP_TILES):
                 nc.vector.bn_aggr(out=mean_var[:, j, :], in_=stats[:, j].rearrange("p h c -> p (h c)"))
@@ -125,7 +126,8 @@ def tile_realimagfourvallinear_pa_t_kernel(
         def normalise(g):
             x_hat[g] = work.tile([P, GROUP_TILES, HALVES, D], F32, name="x_hat")
             for j in range(GROUP_TILES):
-                nc.gpsimd.tensor_scalar(
+                engine = nc.vector if j < VECTOR_NORM_TILES else nc.gpsimd
+                engine.tensor_scalar(
                     out=x_hat[g][:, j], in0=x_tiles[g][:, :, j, :],
                     scalar1=neg_mean[g][:, j : j + 1], scalar2=rstd[g][:, j : j + 1], op0=ALU.add, op1=ALU.mult,
                 )
@@ -149,9 +151,9 @@ def tile_realimagfourvallinear_pa_t_kernel(
             side_by_side = grouped[g, h][:].rearrange("p (c i) t -> p c t i", i=4)
             plane_by_plane = planes[g, h][:].rearrange("p t (c i) -> p c t i", i=4)
             if h == 0:
-                nc.vector.tensor_copy(out=side_by_side, in_=plane_by_plane)
-            else:
                 nc.scalar.copy(out=side_by_side, in_=plane_by_plane)
+            else:
+                nc.vector.tensor_copy(out=side_by_side, in_=plane_by_plane)
 
         def quantise(g):
             codes[g] = work.tile([P, HALVES, GROUP_ROWS], U32, align_bytes=64, name="codes")
@@ -197,22 +199,21 @@ def tile_realimagfourvallinear_pa_t_kernel(
 
         with tc.manual_schedule():
             for s in range(-2, GROUPS + 2):
-                if in_range(s - 1):
-                    regroup(s - 1, 0)
                 if in_range(s + 2):
                     statistics(s + 2)
+                if in_range(s + 1):
+                    normalise(s + 1)
                 if in_range(s - 1):
+                    regroup(s - 1, 1)
                     quantise(s - 1)
                 if in_range(s - 2):
                     multiply(s - 2)
                 if in_range(s):
                     transpose_and_affine(s, 0)
+                    regroup(s, 0)
                 if in_range(s - 2):
                     gains_and_store(s - 2)
                 if in_range(s):
                     transpose_and_affine(s, 1)
-                    regroup(s, 1)
-                if in_range(s + 1):
-                    normalise(s + 1)
                 if in_range(s + 2):
                     reciprocal_std(s + 2)

@@ -24,6 +24,7 @@ GROUP_TILES = 4
 GROUP_ROWS = GROUP_TILES * P
 GROUPS = ROWS // GROUP_ROWS
 VECTOR_NORM_TILES = 1
+SCALAR_REGROUP_TILES = 3
 
 FLOPS = 4 * 2 * ROWS * D * N_OUT
 
@@ -134,6 +135,8 @@ def tile_realimagfourvallinear_pa_t_kernel(
 
         def transpose_and_affine(g, h):
             planes[g, h] = work.tile([P, PACK, GROUP_ROWS], BF16, name="planes_%d" % h)
+            if h == 0:
+                grouped[g] = work.tile([P, HALVES, GROUP_ROWS, PACK], BF16, align_bytes=64, name="grouped")
             for t in range(PACK):
                 b = h * PACK + t
                 x_hat_t = t_psum.tile([P, GROUP_ROWS], F32)
@@ -146,24 +149,24 @@ def tile_realimagfourvallinear_pa_t_kernel(
                     scale=affine_cols[:, b : b + 1], bias=affine_cols[:, K_BLOCKS + b : K_BLOCKS + b + 1],
                 )
 
-        def regroup(g, h):
-            grouped[g, h] = work.tile([P, GROUP_ROWS, PACK], BF16, align_bytes=64, name="grouped_%d" % h)
-            side_by_side = grouped[g, h][:].rearrange("p (c i) t -> p c t i", i=4)
-            plane_by_plane = planes[g, h][:].rearrange("p t (c i) -> p c t i", i=4)
-            if h == 0:
-                nc.scalar.copy(out=side_by_side, in_=plane_by_plane)
-            else:
-                nc.vector.tensor_copy(out=side_by_side, in_=plane_by_plane)
+        def regroup(copy, g, h, first_tile, last_tile):
+            rows = slice(first_tile * P, last_tile * P)
+            copy(
+                out=grouped[g][:, h, rows, :].rearrange("p (c i) t -> p c t i", i=4),
+                in_=planes[g, h][:, :, rows].rearrange("p t (c i) -> p c t i", i=4),
+            )
+
+        def scalar_share(g):
+            return SCALAR_REGROUP_TILES if g + 3 < GROUPS else 0
 
         def quantise(g):
             codes[g] = work.tile([P, HALVES, GROUP_ROWS], U32, align_bytes=64, name="codes")
             scales[g] = work.tile([P, HALVES, GROUP_ROWS], U8, align_bytes=64, name="scales")
-            for h in range(HALVES):
-                nc.vector.quantize_mx(
-                    out=codes[g][:, h, :].bitcast(FP8X4),
-                    scales=scales[g][:, h, :],
-                    in_=grouped[g, h][:].rearrange("p r t -> p (r t)"),
-                )
+            nc.vector.quantize_mx(
+                out=codes[g][:].rearrange("p h r -> p (h r)").bitcast(FP8X4),
+                scales=scales[g][:].rearrange("p h r -> p (h r)"),
+                in_=grouped[g][:].rearrange("p h r t -> p (h r t)"),
+            )
 
         def multiply(g):
             y_ps[g] = []
@@ -201,16 +204,19 @@ def tile_realimagfourvallinear_pa_t_kernel(
             for s in range(-2, GROUPS + 2):
                 if in_range(s + 2):
                     statistics(s + 2)
+                if in_range(s - 1):
+                    regroup(nc.vector.tensor_copy, s - 1, 0, scalar_share(s - 1), GROUP_TILES)
+                    regroup(nc.vector.tensor_copy, s - 1, 1, 0, GROUP_TILES)
                 if in_range(s + 1):
                     normalise(s + 1)
                 if in_range(s - 1):
-                    regroup(s - 1, 1)
                     quantise(s - 1)
                 if in_range(s - 2):
                     multiply(s - 2)
                 if in_range(s):
                     transpose_and_affine(s, 0)
-                    regroup(s, 0)
+                    if scalar_share(s) > 0:
+                        regroup(nc.scalar.copy, s, 0, 0, scalar_share(s))
                 if in_range(s - 2):
                     gains_and_store(s - 2)
                 if in_range(s):

from contextlib import ExitStack

import concourse.mybir as mybir
from concourse.masks import make_identity

F32 = mybir.dt.float32
BF16 = mybir.dt.bfloat16
U32 = mybir.dt.uint32
U8 = mybir.dt.uint8
FP8X4 = mybir.dt.float8_e4m3fn_x4
ACT = mybir.ActivationFunctionType
ALU = mybir.AluOpType

P = 128
PACK = 4
ROWS = 4 * 2048
D = 512
N_OUT = 128
HALVES = 2
K_BLOCKS = HALVES * D // P
EPS = 1e-6

GROUP_TILES = 4
GROUP_ROWS = GROUP_TILES * P
GROUPS = ROWS // GROUP_ROWS
VECTOR_NORM_TILES = 1
SCALAR_REGROUP_TILES = 3

FLOPS = 4 * 2 * ROWS * D * N_OUT


def tile_realimagfourvallinear_pa_t_kernel(
    tc, x_real, x_imag, qw_re, qw_im, gamma, beta, s_re, s_im, out_0, out_1
):
    nc = tc.nc
    x_views = [
        x.flatten_outer_dims().rearrange("(g p j) k -> g p j k", p=P, j=GROUP_TILES)
        for x in (x_real, x_imag)
    ]
    y_views = [
        y.flatten_outer_dims().rearrange("(g p j) n -> g p j n", p=P, j=GROUP_TILES)
        for y in (out_0, out_1)
    ]

    with ExitStack() as ctx:
        const = ctx.enter_context(tc.tile_pool(name="const", bufs=1))
        x_pool = ctx.enter_context(tc.tile_pool(name="x_pool", bufs=GROUPS))

        x_tiles = []
        for g in range(GROUPS):
            x_sb = x_pool.tile([P, HALVES, GROUP_TILES, D], BF16)
            for h in range(HALVES):
                nc.sync.dma_start(out=x_sb[:, h], in_=x_views[h][g])
            x_tiles.append(x_sb)

        ident_f32 = const.tile([P, P], F32)
        make_identity(nc, ident_f32[:])
        minus_half = const.tile([P, GROUP_TILES], F32)
        nc.vector.memset(minus_half[:], -0.5)
        gain_cols = const.tile([P, HALVES], F32)
        affine_cols = const.tile([P, 2 * K_BLOCKS], F32)
        w_codes = const.tile([P, HALVES * 2 * N_OUT], U32, align_bytes=64)
        w_scales = const.tile([P, HALVES * 2 * N_OUT], U8, align_bytes=64)

        with tc.tile_pool(name="setup", bufs=1) as setup, tc.psum_pool(name="setup_psum", bufs=1) as setup_psum:
            ident_bf16 = setup.tile([P, P], BF16)
            make_identity(nc, ident_bf16[:])

            s_re_bf16 = setup.tile([P, 1], BF16)
            s_im_bf16 = setup.tile([P, 1], BF16)
            nc.scalar.dma_start(out=s_re_bf16[:], in_=s_re.partition_broadcast(P))
            nc.scalar.dma_start(out=s_im_bf16[:], in_=s_im.partition_broadcast(P))
            nc.vector.tensor_copy(out=gain_cols[:, 0:1], in_=s_re_bf16[:])
            nc.vector.tensor_copy(out=gain_cols[:, 1:2], in_=s_im_bf16[:])

            affine_rows = setup.tile([P, P], BF16)
            nc.vector.memset(affine_rows[:], 0.0)
            nc.scalar.dma_start(out=affine_rows[0:K_BLOCKS, :], in_=gamma.rearrange("(b c) -> b c", c=P))
            nc.scalar.dma_start(out=affine_rows[K_BLOCKS : 2 * K_BLOCKS, :], in_=beta.rearrange("(b c) -> b c", c=P))
            affine_t = setup_psum.tile([P, P], BF16)
            nc.tensor.transpose(affine_t[:], affine_rows[:], ident_bf16[:])
            nc.vector.tensor_copy(out=affine_cols[:], in_=affine_t[:, 0 : 2 * K_BLOCKS])

            w_t = []
            for w in (qw_re, qw_im):
                w_sb = setup.tile([P, D], BF16, name="w_sb", bufs=2)
                nc.scalar.dma_start(out=w_sb[:], in_=w)
                w_ps = setup_psum.tile([P, PACK, N_OUT], BF16, name="w_ps", bufs=2)
                for t in range(PACK):
                    nc.tensor.transpose(w_ps[:, t, :], w_sb[:, t * P : (t + 1) * P], ident_bf16[:])
                w_t.append(w_ps[:].rearrange("p t n -> p n t"))
            w_grouped = setup.tile([P, HALVES * 2, N_OUT, PACK], BF16, align_bytes=64)
            nc.vector.tensor_copy(out=w_grouped[:, 0], in_=w_t[0])
            nc.vector.tensor_copy(out=w_grouped[:, 1], in_=w_t[1])
            nc.vector.tensor_scalar_mul(out=w_grouped[:, 2], in0=w_t[1], scalar1=-1.0)
            nc.vector.tensor_copy(out=w_grouped[:, 3], in_=w_t[0])
            nc.vector.quantize_mx(
                out=w_codes[:].bitcast(FP8X4),
                scales=w_scales[:],
                in_=w_grouped[:].rearrange("p q n t -> p (q n t)"),
            )

        small = ctx.enter_context(tc.tile_pool(name="small", bufs=4))
        work = ctx.enter_context(tc.tile_pool(name="work", bufs=2))
        t_psum = ctx.enter_context(tc.psum_pool(name="t_psum", bufs=6))
        y_psum = ctx.enter_context(tc.psum_pool(name="y_psum", bufs=2))

        neg_mean, var_eps, rstd, x_hat, planes, grouped, codes, scales, y_ps = ({} for i in range(9))

        def statistics(g):
            stats = small.tile([P, GROUP_TILES, HALVES, 6], F32)
            mean_var = small.tile([P, GROUP_TILES, 2], F32)
            for h in range(HALVES):
                for j in range(GROUP_TILES):
                    nc.vector.bn_stats(out=stats[:, j, h, :], in_=x_tiles[g][:, h, j, :])
            for j in range(GROUP_TILES):
                nc.vector.bn_aggr(out=mean_var[:, j, :], in_=stats[:, j].rearrange("p h c -> p (h c)"))
            neg_mean[g] = small.tile([P, GROUP_TILES], F32, name="neg_mean")
            nc.vector.tensor_scalar_mul(out=neg_mean[g][:], in0=mean_var[:, :, 0], scalar1=-1.0)
            var_eps[g] = small.tile([P, GROUP_TILES], F32, name="var_eps")
            nc.vector.tensor_scalar_add(out=var_eps[g][:], in0=mean_var[:, :, 1], scalar1=EPS)

        def reciprocal_std(g):
            rstd[g] = small.tile([P, GROUP_TILES], F32, name="rstd")
            nc.gpsimd.tensor_tensor(out=rstd[g][:], in0=var_eps[g][:], in1=minus_half[:], op=ALU.pow)

        def normalise(g):
            x_hat[g] = work.tile([P, GROUP_TILES, HALVES, D], F32, name="x_hat")
            for j in range(GROUP_TILES):
                engine = nc.vector if j < VECTOR_NORM_TILES else nc.gpsimd
                engine.tensor_scalar(
                    out=x_hat[g][:, j], in0=x_tiles[g][:, :, j, :],
                    scalar1=neg_mean[g][:, j : j + 1], scalar2=rstd[g][:, j : j + 1], op0=ALU.add, op1=ALU.mult,
                )

        def transpose_and_affine(g, h):
            planes[g, h] = work.tile([P, PACK, GROUP_ROWS], BF16, name="planes_%d" % h)
            if h == 0:
                grouped[g] = work.tile([P, HALVES, GROUP_ROWS, PACK], BF16, align_bytes=64, name="grouped")
            for t in range(PACK):
                b = h * PACK + t
                x_hat_t = t_psum.tile([P, GROUP_ROWS], F32)
                for j in range(GROUP_TILES):
                    nc.tensor.transpose(
                        x_hat_t[:, j * P : (j + 1) * P], x_hat[g][:, j, h, t * P : (t + 1) * P], ident_f32[:]
                    )
                nc.scalar.activation(
                    out=planes[g, h][:, t, :], in_=x_hat_t[:], func=ACT.Identity,
                    scale=affine_cols[:, b : b + 1], bias=affine_cols[:, K_BLOCKS + b : K_BLOCKS + b + 1],
                )

        def regroup(copy, g, h, first_tile, last_tile):
            rows = slice(first_tile * P, last_tile * P)
            copy(
                out=grouped[g][:, h, rows, :].rearrange("p (c i) t -> p c t i", i=4),
                in_=planes[g, h][:, :, rows].rearrange("p t (c i) -> p c t i", i=4),
            )

        def scalar_share(g):
            return SCALAR_REGROUP_TILES if g + 3 < GROUPS else 0

        def quantise(g):
            codes[g] = work.tile([P, HALVES, GROUP_ROWS], U32, align_bytes=64, name="codes")
            scales[g] = work.tile([P, HALVES, GROUP_ROWS], U8, align_bytes=64, name="scales")
            nc.vector.quantize_mx(
                out=codes[g][:].rearrange("p h r -> p (h r)").bitcast(FP8X4),
                scales=scales[g][:].rearrange("p h r -> p (h r)"),
                in_=grouped[g][:].rearrange("p h r t -> p (h r t)"),
            )

        def multiply(g):
            y_ps[g] = []
            for pair in range(GROUP_TILES // 2):
                y_pair = y_psum.tile([P, 2, HALVES * N_OUT], F32)
                for i in range(2):
                    rows = slice((2 * pair + i) * P, (2 * pair + i + 1) * P)
                    for h in range(HALVES):
                        cols = slice(h * 2 * N_OUT, (h + 1) * 2 * N_OUT)
                        nc.tensor.matmul_mx(
                            out=y_pair[:, i, :],
                            lhsT=codes[g][:, h, rows].bitcast(FP8X4),
                            lhsT_scale=scales[g][:, h, rows],
                            rhs=w_codes[:, cols].bitcast(FP8X4),
                            rhs_scale=w_scales[:, cols],
                            start=(h == 0),
                            stop=(h == HALVES - 1),
                        )
                y_ps[g].append(y_pair)

        def gains_and_store(g):
            for c in range(HALVES):
                y_sb = work.tile([P, GROUP_TILES, N_OUT], F32, name="y_sb_%d" % c)
                for pair in range(GROUP_TILES // 2):
                    nc.scalar.activation(
                        out=y_sb[:, 2 * pair : 2 * pair + 2, :], in_=y_ps[g][pair][:, :, c * N_OUT : (c + 1) * N_OUT],
                        func=ACT.Copy, scale=gain_cols[:, c : c + 1],
                    )
                nc.sync.dma_start(out=y_views[c][g], in_=y_sb[:])

        def in_range(g):
            return 0 <= g < GROUPS

        with tc.manual_schedule():
            for s in range(-2, GROUPS + 2):
                if in_range(s + 2):
                    statistics(s + 2)
                if in_range(s - 1):
                    regroup(nc.vector.tensor_copy, s - 1, 0, scalar_share(s - 1), GROUP_TILES)
                    regroup(nc.vector.tensor_copy, s - 1, 1, 0, GROUP_TILES)
                if in_range(s + 1):
                    normalise(s + 1)
                if in_range(s - 1):
                    quantise(s - 1)
                if in_range(s - 2):
                    multiply(s - 2)
                if in_range(s):
                    transpose_and_affine(s, 0)
                    if scalar_share(s) > 0:
                        regroup(nc.scalar.copy, s, 0, 0, scalar_share(s))
                if in_range(s - 2):
                    gains_and_store(s - 2)
                if in_range(s):
                    transpose_and_affine(s, 1)
                if in_range(s + 2):
                    reciprocal_std(s + 2)
